import numpy as np
import ml_dtypes

BF16 = ml_dtypes.bfloat16


def bf(x):
    return np.asarray(x, np.float32).astype(BF16)


def f32(x):
    return np.asarray(x, np.float32)


def f64(x):
    return np.asarray(x).astype(np.float64)


def striped(idx):
    return np.tile(idx.reshape(-1, 16).T, (8, 1))


C, S, N, P = 128, 2048, 256, 1024
FEAT_SCALE, MEAN_SCALE, BASE_SCALE = 0.8, 0.25, 0.4


def setup_inputs():
    return {"base": f32(BASE_SCALE * np.random.standard_normal((C, S))), "feat": bf(FEAT_SCALE * np.random.standard_normal((C, P))), "mean": bf(MEAN_SCALE * np.random.standard_normal((C, N))), "adjust": f32(np.random.standard_normal((P, N))), "offs": striped(np.random.permutation(S)[:N])}


def reference(base, feat, mean, adjust, offs):
    idx = offs[:16].T.reshape(-1)
    f, m = f64(feat), f64(mean)
    logit = 2.0 * (f.T @ m) - (m * m).sum(axis=0)[None, :] - f64(adjust)
    e = np.exp(logit - logit.max(axis=1, keepdims=True))
    post = e / e.sum(axis=1, keepdims=True)
    num = f @ post
    r = 1.0 / post.sum(axis=0)
    out = f64(base).copy()
    out[:, idx] = num * r[None, :]
    return out

@@ -1,0 +1,99 @@
+import concourse.mybir as mybir
+from concourse.masks import make_identity
+
+F32 = mybir.dt.float32
+BF16 = mybir.dt.bfloat16
+U16 = mybir.dt.uint16
+ALU = mybir.AluOpType
+ACT = mybir.ActivationFunctionType
+
+C = 128
+S = 2048
+N = 256
+P = 1024
+PB = 128
+NB = P // PB
+STORE_COLS = 512
+
+FLOPS = 4 * C * P * N
+
+
+def tile_em_step_kernel(tc, base, feat, mean, adjust, offs, out):
+    nc = tc.nc
+    with (
+        tc.tile_pool(name="held", bufs=1) as held,
+        tc.tile_pool(name="work", bufs=3) as work,
+        tc.psum_pool(name="logit_banks", bufs=3) as logit_banks,
+        tc.psum_pool(name="flip_banks", bufs=2) as flip_banks,
+        tc.psum_pool(name="sum_banks", bufs=1) as sum_banks,
+    ):
+        offsets = held.tile([C, N // 16], U16, name="offsets")
+        nc.sync.dma_start(offsets[:], offs)
+        mean_sb = held.tile([C, N], BF16, name="mean_sb")
+        nc.sync.dma_start(mean_sb[:], mean)
+        feat_sb = held.tile([C, P], BF16, name="feat_sb")
+        nc.scalar.dma_start(feat_sb[:], feat)
+        adjust_blocks = adjust.rearrange("(b p) j -> b p j", p=PB)
+        adjust_sb = []
+        for b in range(NB):
+            adjust_b = held.tile([PB, N], F32, name=f"adjust{b}")
+            queue = nc.sync if b % 2 == 0 else nc.scalar
+            queue.dma_start(adjust_b[:], adjust_blocks[b])
+            adjust_sb.append(adjust_b)
+        window = held.tile([C, S], F32, name="window")
+        nc.sync.dma_start(window[:, : S // 2], base[:, : S // 2])
+        nc.scalar.dma_start(window[:, S // 2 :], base[:, S // 2 :])
+
+        identity = held.tile([C, C], BF16, name="identity")
+        make_identity(nc, identity[:])
+        minus_ones = held.tile([C, PB], BF16, name="minus_ones")
+        nc.gpsimd.memset(minus_ones[:], -1.0)
+        ones = held.tile([PB, C], BF16, name="ones")
+        nc.gpsimd.memset(ones[:], 1.0)
+        mean_doubled = held.tile([C, N], BF16, name="mean_doubled")
+        nc.vector.tensor_scalar_mul(mean_doubled[:], mean_sb[:], 2.0)
+        mean_squared = held.tile([C, N], BF16, name="mean_squared")
+        nc.vector.tensor_mul(mean_squared[:], mean_sb[:], mean_sb[:])
+
+        num_ps = sum_banks.tile([C, N], F32, name="num_ps")
+        count_ps = sum_banks.tile([C, N], F32, name="count_ps")
+
+        for b in range(NB):
+            pixels = slice(b * PB, (b + 1) * PB)
+
+            logit_ps = logit_banks.tile([PB, N], F32, name="logit_ps")
+            nc.tensor.matmul(logit_ps[:], feat_sb[:, pixels], mean_doubled[:], start=True, stop=False)
+            nc.tensor.matmul(logit_ps[:], minus_ones[:], mean_squared[:], start=False, stop=True)
+
+            flipped_ps = flip_banks.tile([PB, C], BF16, name="flipped_ps")
+            nc.tensor.transpose(flipped_ps[:], feat_sb[:, pixels], identity[:])
+            flipped = work.tile([PB, C], BF16, name="flipped")
+            nc.scalar.copy(flipped[:], flipped_ps[:])
+
+            logit = work.tile([PB, N], F32, name="logit")
+            nc.vector.tensor_tensor(logit[:], logit_ps[:], adjust_sb[b][:], ALU.subtract)
+            minus_top = work.tile([PB, 1], F32, name="minus_top")
+            nc.vector.tensor_reduce(minus_top[:], logit[:], mybir.AxisListType.X, ALU.max, negate=True)
+
+            grown = work.tile([PB, N], F32, name="grown")
+            row_sum = work.tile([PB, 1], F32, name="row_sum")
+            nc.scalar.activation(grown[:], logit[:], ACT.Exp, bias=minus_top[:], scale=1.0, accum_out=row_sum[:])
+
+            row_scale = work.tile([PB, 1], F32, name="row_scale")
+            nc.vector.reciprocal(row_scale[:], row_sum[:])
+            post = work.tile([PB, N], BF16, name="post")
+            nc.gpsimd.tensor_scalar(post[:], grown[:], row_scale[:], 1.0, ALU.mult, ALU.mult)
+
+            nc.tensor.matmul(count_ps[:], ones[:], post[:], start=(b == 0), stop=(b == NB - 1))
+            nc.tensor.matmul(num_ps[:], flipped[:], post[:], start=(b == 0), stop=(b == NB - 1))
+
+        count_recip = held.tile([C, N], F32, name="count_recip")
+        nc.vector.reciprocal(count_recip[:], count_ps[:])
+        num_sb = held.tile([C, N], F32, name="num_sb")
+        nc.scalar.copy(num_sb[:], num_ps[:])
+
+        nc.vector.tensor_tensor(window[:].indirect(offsets[:]), num_sb[:], count_recip[:], ALU.mult)
+
+        for first in range(0, S, STORE_COLS):
+            queue = nc.sync if (first // STORE_COLS) % 2 == 0 else nc.scalar
+            queue.dma_start(out[:, first : first + STORE_COLS], window[:, first : first + STORE_COLS])

@@ -22,7 +22,8 @@ def tile_em_step_kernel(tc, base, feat, mean, adjust, offs, out):
     nc = tc.nc
     with (
         tc.tile_pool(name="held", bufs=1) as held,
-        tc.tile_pool(name="work", bufs=3) as work,
+        tc.tile_pool(name="work", bufs=4) as work,
+        tc.tile_pool(name="flips", bufs=NB) as flips,
         tc.psum_pool(name="logit_banks", bufs=3) as logit_banks,
         tc.psum_pool(name="flip_banks", bufs=2) as flip_banks,
         tc.psum_pool(name="sum_banks", bufs=1) as sum_banks,
@@ -67,7 +68,7 @@ def tile_em_step_kernel(tc, base, feat, mean, adjust, offs, out):
 
             flipped_ps = flip_banks.tile([PB, C], BF16, name="flipped_ps")
             nc.tensor.transpose(flipped_ps[:], feat_sb[:, pixels], identity[:])
-            flipped = work.tile([PB, C], BF16, name="flipped")
+            flipped = flips.tile([PB, C], BF16, name="flipped")
             nc.scalar.copy(flipped[:], flipped_ps[:])
 
             logit = work.tile([PB, N], F32, name="logit")

@@ -13,6 +13,8 @@ N = 256
 P = 1024
 PB = 128
 NB = P // PB
+CODES_HALF = 128
+HALVES = N // CODES_HALF
 STORE_COLS = 512
 
 FLOPS = 4 * C * P * N
@@ -28,36 +30,42 @@ def tile_em_step_kernel(tc, base, feat, mean, adjust, offs, out):
         tc.psum_pool(name="flip_banks", bufs=2) as flip_banks,
         tc.psum_pool(name="sum_banks", bufs=1) as sum_banks,
     ):
-        offsets = held.tile([C, N // 16], U16, name="offsets")
-        nc.sync.dma_start(offsets[:], offs)
         mean_sb = held.tile([C, N], BF16, name="mean_sb")
         nc.sync.dma_start(mean_sb[:], mean)
         feat_sb = held.tile([C, P], BF16, name="feat_sb")
-        nc.scalar.dma_start(feat_sb[:], feat)
-        adjust_blocks = adjust.rearrange("(b p) j -> b p j", p=PB)
+        nc.sync.dma_start(feat_sb[:], feat)
+        adjust_pairs = adjust.rearrange("(g h p) j -> g p h j", h=2, p=PB)
         adjust_sb = []
-        for b in range(NB):
-            adjust_b = held.tile([PB, N], F32, name=f"adjust{b}")
-            queue = nc.sync if b % 2 == 0 else nc.scalar
-            queue.dma_start(adjust_b[:], adjust_blocks[b])
-            adjust_sb.append(adjust_b)
+        for g in range(NB // 2):
+            adjust_pair = held.tile([PB, 2, N], F32, name=f"adjust_pair{g}")
+            nc.sync.dma_start(adjust_pair[:], adjust_pairs[g])
+            adjust_sb.append(adjust_pair[:, 0, :])
+            adjust_sb.append(adjust_pair[:, 1, :])
+        offsets = held.tile([C, N // 16], U16, name="offsets")
+        nc.sync.dma_start(offsets[:], offs)
         window = held.tile([C, S], F32, name="window")
-        nc.sync.dma_start(window[:, : S // 2], base[:, : S // 2])
-        nc.scalar.dma_start(window[:, S // 2 :], base[:, S // 2 :])
+        nc.sync.dma_start(window[:], base)
+
+        one_f32 = held.tile([C, 1], F32, name="one_f32")
+        nc.vector.memset(one_f32[:], 1.0)
+        table_warmer = held.tile([C, 1], F32, name="table_warmer")
+        nc.scalar.activation(table_warmer[:], one_f32[:], ACT.Exp)
 
         identity = held.tile([C, C], BF16, name="identity")
         make_identity(nc, identity[:])
         minus_ones = held.tile([C, PB], BF16, name="minus_ones")
         nc.gpsimd.memset(minus_ones[:], -1.0)
-        ones = held.tile([PB, C], BF16, name="ones")
-        nc.gpsimd.memset(ones[:], 1.0)
+        one_column = held.tile([PB, 1], BF16, name="one_column")
+        nc.gpsimd.memset(one_column[:], 1.0)
+        identity_f32 = held.tile([C, C], F32, name="identity_f32")
+        make_identity(nc, identity_f32[:])
         mean_doubled = held.tile([C, N], BF16, name="mean_doubled")
         nc.vector.tensor_scalar_mul(mean_doubled[:], mean_sb[:], 2.0)
         mean_squared = held.tile([C, N], BF16, name="mean_squared")
         nc.vector.tensor_mul(mean_squared[:], mean_sb[:], mean_sb[:])
 
         num_ps = sum_banks.tile([C, N], F32, name="num_ps")
-        count_ps = sum_banks.tile([C, N], F32, name="count_ps")
+        count_ps = sum_banks.tile([CODES_HALF, HALVES], F32, name="count_ps")
 
         for b in range(NB):
             pixels = slice(b * PB, (b + 1) * PB)
@@ -72,7 +80,7 @@ def tile_em_step_kernel(tc, base, feat, mean, adjust, offs, out):
             nc.scalar.copy(flipped[:], flipped_ps[:])
 
             logit = work.tile([PB, N], F32, name="logit")
-            nc.vector.tensor_tensor(logit[:], logit_ps[:], adjust_sb[b][:], ALU.subtract)
+            nc.vector.tensor_tensor(logit[:], logit_ps[:], adjust_sb[b], ALU.subtract)
             minus_top = work.tile([PB, 1], F32, name="minus_top")
             nc.vector.tensor_reduce(minus_top[:], logit[:], mybir.AxisListType.X, ALU.max, negate=True)
 
@@ -83,17 +91,37 @@ def tile_em_step_kernel(tc, base, feat, mean, adjust, offs, out):
             row_scale = work.tile([PB, 1], F32, name="row_scale")
             nc.vector.reciprocal(row_scale[:], row_sum[:])
             post = work.tile([PB, N], BF16, name="post")
-            nc.gpsimd.tensor_scalar(post[:], grown[:], row_scale[:], 1.0, ALU.mult, ALU.mult)
+            if b < NB - 1:
+                nc.gpsimd.tensor_scalar(post[:], grown[:], row_scale[:], 1.0, ALU.mult, ALU.mult)
+            else:
+                nc.vector.tensor_scalar_mul(post[:], grown[:], row_scale[:])
 
-            nc.tensor.matmul(count_ps[:], ones[:], post[:], start=(b == 0), stop=(b == NB - 1))
+            for h in range(HALVES):
+                nc.tensor.matmul(
+                    count_ps[:, h : h + 1],
+                    post[:, h * CODES_HALF : (h + 1) * CODES_HALF],
+                    one_column[:],
+                    start=(b == 0 and h == 0),
+                    stop=(b == NB - 1 and h == HALVES - 1),
+                )
             nc.tensor.matmul(num_ps[:], flipped[:], post[:], start=(b == 0), stop=(b == NB - 1))
 
-        count_recip = held.tile([C, N], F32, name="count_recip")
-        nc.vector.reciprocal(count_recip[:], count_ps[:])
+        r_column = held.tile([CODES_HALF, HALVES], F32, name="r_column")
+        nc.vector.reciprocal(r_column[:], count_ps[:])
         num_sb = held.tile([C, N], F32, name="num_sb")
         nc.scalar.copy(num_sb[:], num_ps[:])
+        r_rows = sum_banks.tile([C, N], F32, name="r_rows")
+        for h in range(HALVES):
+            nc.tensor.transpose(
+                r_rows[:, h * CODES_HALF : (h + 1) * CODES_HALF],
+                r_column[:, h : h + 1].to_broadcast([CODES_HALF, C]),
+                identity_f32[:],
+            )
 
-        nc.vector.tensor_tensor(window[:].indirect(offsets[:]), num_sb[:], count_recip[:], ALU.mult)
+        r_sb = held.tile([C, N], F32, name="r_sb")
+        nc.vector.tensor_copy(r_sb[:], r_rows[:])
+
+        nc.vector.tensor_tensor(window[:].indirect(offsets[:]), num_sb[:], r_sb[:], ALU.mult)
 
         for first in range(0, S, STORE_COLS):
             queue = nc.sync if (first // STORE_COLS) % 2 == 0 else nc.scalar

@@ -31,16 +31,15 @@ def tile_em_step_kernel(tc, base, feat, mean, adjust, offs, out):
         tc.psum_pool(name="sum_banks", bufs=1) as sum_banks,
     ):
         mean_sb = held.tile([C, N], BF16, name="mean_sb")
-        nc.sync.dma_start(mean_sb[:], mean)
         feat_sb = held.tile([C, P], BF16, name="feat_sb")
-        nc.sync.dma_start(feat_sb[:], feat)
-        adjust_pairs = adjust.rearrange("(g h p) j -> g p h j", h=2, p=PB)
-        adjust_sb = []
-        for g in range(NB // 2):
-            adjust_pair = held.tile([PB, 2, N], F32, name=f"adjust_pair{g}")
-            nc.sync.dma_start(adjust_pair[:], adjust_pairs[g])
-            adjust_sb.append(adjust_pair[:, 0, :])
-            adjust_sb.append(adjust_pair[:, 1, :])
+        adjust_sb = held.tile([PB, NB, N], F32, name="adjust_sb")
+        adjust_blocks = adjust.rearrange("(b p) j -> p b j", p=PB)
+        nc.sync.dma_start(mean_sb[:], mean)
+        nc.sync.dma_start(feat_sb[:, : 2 * PB], feat[:, : 2 * PB])
+        nc.sync.dma_start(adjust_sb[:, 0:2, :], adjust_blocks[:, 0:2, :])
+        nc.sync.dma_start(feat_sb[:, 2 * PB :], feat[:, 2 * PB :])
+        nc.sync.dma_start(adjust_sb[:, 2:4, :], adjust_blocks[:, 2:4, :])
+        nc.sync.dma_start(adjust_sb[:, 4:NB, :], adjust_blocks[:, 4:NB, :])
         offsets = held.tile([C, N // 16], U16, name="offsets")
         nc.sync.dma_start(offsets[:], offs)
         window = held.tile([C, S], F32, name="window")
@@ -80,7 +79,7 @@ def tile_em_step_kernel(tc, base, feat, mean, adjust, offs, out):
             nc.scalar.copy(flipped[:], flipped_ps[:])
 
             logit = work.tile([PB, N], F32, name="logit")
-            nc.vector.tensor_tensor(logit[:], logit_ps[:], adjust_sb[b], ALU.subtract)
+            nc.vector.tensor_tensor(logit[:], logit_ps[:], adjust_sb[:, b, :], ALU.subtract)
             minus_top = work.tile([PB, 1], F32, name="minus_top")
             nc.vector.tensor_reduce(minus_top[:], logit[:], mybir.AxisListType.X, ALU.max, negate=True)
 

@@ -52,14 +52,12 @@ def tile_em_step_kernel(tc, base, feat, mean, adjust, offs, out):
 
         identity = held.tile([C, C], BF16, name="identity")
         make_identity(nc, identity[:])
-        minus_ones = held.tile([C, PB], BF16, name="minus_ones")
-        nc.gpsimd.memset(minus_ones[:], -1.0)
+        minus_halves = held.tile([C, PB], BF16, name="minus_halves")
+        nc.gpsimd.memset(minus_halves[:], -0.5)
         one_column = held.tile([PB, 1], BF16, name="one_column")
         nc.gpsimd.memset(one_column[:], 1.0)
         identity_f32 = held.tile([C, C], F32, name="identity_f32")
         make_identity(nc, identity_f32[:])
-        mean_doubled = held.tile([C, N], BF16, name="mean_doubled")
-        nc.vector.tensor_scalar_mul(mean_doubled[:], mean_sb[:], 2.0)
         mean_squared = held.tile([C, N], BF16, name="mean_squared")
         nc.vector.tensor_mul(mean_squared[:], mean_sb[:], mean_sb[:])
 
@@ -69,9 +67,9 @@ def tile_em_step_kernel(tc, base, feat, mean, adjust, offs, out):
         for b in range(NB):
             pixels = slice(b * PB, (b + 1) * PB)
 
-            logit_ps = logit_banks.tile([PB, N], F32, name="logit_ps")
-            nc.tensor.matmul(logit_ps[:], feat_sb[:, pixels], mean_doubled[:], start=True, stop=False)
-            nc.tensor.matmul(logit_ps[:], minus_ones[:], mean_squared[:], start=False, stop=True)
+            half_ps = logit_banks.tile([PB, N], F32, name="half_ps")
+            nc.tensor.matmul(half_ps[:], feat_sb[:, pixels], mean_sb[:], start=True, stop=False)
+            nc.tensor.matmul(half_ps[:], minus_halves[:], mean_squared[:], start=False, stop=True)
 
             flipped_ps = flip_banks.tile([PB, C], BF16, name="flipped_ps")
             nc.tensor.transpose(flipped_ps[:], feat_sb[:, pixels], identity[:])
@@ -79,7 +77,7 @@ def tile_em_step_kernel(tc, base, feat, mean, adjust, offs, out):
             nc.scalar.copy(flipped[:], flipped_ps[:])
 
             logit = work.tile([PB, N], F32, name="logit")
-            nc.vector.tensor_tensor(logit[:], logit_ps[:], adjust_sb[:, b, :], ALU.subtract)
+            nc.vector.scalar_tensor_tensor(logit[:], half_ps[:], 2.0, adjust_sb[:, b, :], ALU.mult, ALU.subtract)
             minus_top = work.tile([PB, 1], F32, name="minus_top")
             nc.vector.tensor_reduce(minus_top[:], logit[:], mybir.AxisListType.X, ALU.max, negate=True)
 

@@ -88,7 +88,9 @@ def tile_em_step_kernel(tc, base, feat, mean, adjust, offs, out):
             row_scale = work.tile([PB, 1], F32, name="row_scale")
             nc.vector.reciprocal(row_scale[:], row_sum[:])
             post = work.tile([PB, N], BF16, name="post")
-            if b < NB - 1:
+            if b % 3 == 2:
+                nc.scalar.activation(post[:], grown[:], ACT.Copy, scale=row_scale[:])
+            elif b < NB - 1:
                 nc.gpsimd.tensor_scalar(post[:], grown[:], row_scale[:], 1.0, ALU.mult, ALU.mult)
             else:
                 nc.vector.tensor_scalar_mul(post[:], grown[:], row_scale[:])

@@ -108,17 +108,15 @@ def tile_em_step_kernel(tc, base, feat, mean, adjust, offs, out):
         r_column = held.tile([CODES_HALF, HALVES], F32, name="r_column")
         nc.vector.reciprocal(r_column[:], count_ps[:])
         num_sb = held.tile([C, N], F32, name="num_sb")
-        nc.scalar.copy(num_sb[:], num_ps[:])
-        r_rows = sum_banks.tile([C, N], F32, name="r_rows")
-        for h in range(HALVES):
-            nc.tensor.transpose(
-                r_rows[:, h * CODES_HALF : (h + 1) * CODES_HALF],
-                r_column[:, h : h + 1].to_broadcast([CODES_HALF, C]),
-                identity_f32[:],
-            )
-
+        nc.vector.tensor_copy(num_sb[:], num_ps[:])
         r_sb = held.tile([C, N], F32, name="r_sb")
-        nc.vector.tensor_copy(r_sb[:], r_rows[:])
+        for h in range(HALVES):
+            r_rows = flip_banks.tile([C, CODES_HALF], F32, name="r_rows", tag="flipped_ps")
+            nc.tensor.transpose(r_rows[:], r_column[:, h : h + 1].to_broadcast([CODES_HALF, C]), identity_f32[:])
+            if h == 0:
+                nc.vector.tensor_copy(r_sb[:, :CODES_HALF], r_rows[:])
+            else:
+                nc.scalar.copy(r_sb[:, CODES_HALF:], r_rows[:])
 
         nc.vector.tensor_tensor(window[:].indirect(offsets[:]), num_sb[:], r_sb[:], ALU.mult)
 

@@ -45,11 +45,6 @@ def tile_em_step_kernel(tc, base, feat, mean, adjust, offs, out):
         window = held.tile([C, S], F32, name="window")
         nc.sync.dma_start(window[:], base)
 
-        one_f32 = held.tile([C, 1], F32, name="one_f32")
-        nc.vector.memset(one_f32[:], 1.0)
-        table_warmer = held.tile([C, 1], F32, name="table_warmer")
-        nc.scalar.activation(table_warmer[:], one_f32[:], ACT.Exp)
-
         identity = held.tile([C, C], BF16, name="identity")
         make_identity(nc, identity[:])
         minus_halves = held.tile([C, PB], BF16, name="minus_halves")

@@ -33,13 +33,14 @@ def tile_em_step_kernel(tc, base, feat, mean, adjust, offs, out):
         mean_sb = held.tile([C, N], BF16, name="mean_sb")
         feat_sb = held.tile([C, P], BF16, name="feat_sb")
         adjust_sb = held.tile([PB, NB, N], F32, name="adjust_sb")
-        adjust_blocks = adjust.rearrange("(b p) j -> p b j", p=PB)
+        adjust_pairs = adjust.rearrange("(g p i) j -> p g i j", p=PB, i=2)
+        adjust_sb_pairs = adjust_sb[:].rearrange("p (g i) j -> p g i j", i=2)
         nc.sync.dma_start(mean_sb[:], mean)
         nc.sync.dma_start(feat_sb[:, : 2 * PB], feat[:, : 2 * PB])
-        nc.sync.dma_start(adjust_sb[:, 0:2, :], adjust_blocks[:, 0:2, :])
+        nc.sync.dma_start(adjust_sb_pairs[:, 0:1], adjust_pairs[:, 0:1])
         nc.sync.dma_start(feat_sb[:, 2 * PB :], feat[:, 2 * PB :])
-        nc.sync.dma_start(adjust_sb[:, 2:4, :], adjust_blocks[:, 2:4, :])
-        nc.sync.dma_start(adjust_sb[:, 4:NB, :], adjust_blocks[:, 4:NB, :])
+        nc.sync.dma_start(adjust_sb_pairs[:, 1:2], adjust_pairs[:, 1:2])
+        nc.sync.dma_start(adjust_sb_pairs[:, 2:], adjust_pairs[:, 2:])
         offsets = held.tile([C, N // 16], U16, name="offsets")
         nc.sync.dma_start(offsets[:], offs)
         window = held.tile([C, S], F32, name="window")
@@ -60,7 +61,8 @@ def tile_em_step_kernel(tc, base, feat, mean, adjust, offs, out):
         count_ps = sum_banks.tile([CODES_HALF, HALVES], F32, name="count_ps")
 
         for b in range(NB):
-            pixels = slice(b * PB, (b + 1) * PB)
+            first_pixel = b // 2 * 2 * PB + b % 2
+            pixels = slice(first_pixel, first_pixel + 2 * PB - 1, 2)
 
             half_ps = logit_banks.tile([PB, N], F32, name="half_ps")
             nc.tensor.matmul(half_ps[:], feat_sb[:, pixels], mean_sb[:], start=True, stop=False)

@@ -110,10 +110,7 @@ def tile_em_step_kernel(tc, base, feat, mean, adjust, offs, out):
         for h in range(HALVES):
             r_rows = flip_banks.tile([C, CODES_HALF], F32, name="r_rows", tag="flipped_ps")
             nc.tensor.transpose(r_rows[:], r_column[:, h : h + 1].to_broadcast([CODES_HALF, C]), identity_f32[:])
-            if h == 0:
-                nc.vector.tensor_copy(r_sb[:, :CODES_HALF], r_rows[:])
-            else:
-                nc.scalar.copy(r_sb[:, CODES_HALF:], r_rows[:])
+            nc.vector.tensor_copy(r_sb[:, h * CODES_HALF : (h + 1) * CODES_HALF], r_rows[:])
 
         nc.vector.tensor_tensor(window[:].indirect(offsets[:]), num_sb[:], r_sb[:], ALU.mult)
 

import concourse.mybir as mybir
from concourse.masks import make_identity

F32 = mybir.dt.float32
BF16 = mybir.dt.bfloat16
U16 = mybir.dt.uint16
ALU = mybir.AluOpType
ACT = mybir.ActivationFunctionType

C = 128
S = 2048
N = 256
P = 1024
PB = 128
NB = P // PB
CODES_HALF = 128
HALVES = N // CODES_HALF
STORE_COLS = 512

FLOPS = 4 * C * P * N


def tile_em_step_kernel(tc, base, feat, mean, adjust, offs, out):
    nc = tc.nc
    with (
        tc.tile_pool(name="held", bufs=1) as held,
        tc.tile_pool(name="work", bufs=4) as work,
        tc.tile_pool(name="flips", bufs=NB) as flips,
        tc.psum_pool(name="logit_banks", bufs=3) as logit_banks,
        tc.psum_pool(name="flip_banks", bufs=2) as flip_banks,
        tc.psum_pool(name="sum_banks", bufs=1) as sum_banks,
    ):
        mean_sb = held.tile([C, N], BF16, name="mean_sb")
        feat_sb = held.tile([C, P], BF16, name="feat_sb")
        adjust_sb = held.tile([PB, NB, N], F32, name="adjust_sb")
        adjust_pairs = adjust.rearrange("(g p i) j -> p g i j", p=PB, i=2)
        adjust_sb_pairs = adjust_sb[:].rearrange("p (g i) j -> p g i j", i=2)
        nc.sync.dma_start(mean_sb[:], mean)
        nc.sync.dma_start(feat_sb[:, : 2 * PB], feat[:, : 2 * PB])
        nc.sync.dma_start(adjust_sb_pairs[:, 0:1], adjust_pairs[:, 0:1])
        nc.sync.dma_start(feat_sb[:, 2 * PB :], feat[:, 2 * PB :])
        nc.sync.dma_start(adjust_sb_pairs[:, 1:2], adjust_pairs[:, 1:2])
        nc.sync.dma_start(adjust_sb_pairs[:, 2:], adjust_pairs[:, 2:])
        offsets = held.tile([C, N // 16], U16, name="offsets")
        nc.sync.dma_start(offsets[:], offs)
        window = held.tile([C, S], F32, name="window")
        nc.sync.dma_start(window[:], base)

        identity = held.tile([C, C], BF16, name="identity")
        make_identity(nc, identity[:])
        minus_halves = held.tile([C, PB], BF16, name="minus_halves")
        nc.gpsimd.memset(minus_halves[:], -0.5)
        one_column = held.tile([PB, 1], BF16, name="one_column")
        nc.gpsimd.memset(one_column[:], 1.0)
        identity_f32 = held.tile([C, C], F32, name="identity_f32")
        make_identity(nc, identity_f32[:])
        mean_squared = held.tile([C, N], BF16, name="mean_squared")
        nc.vector.tensor_mul(mean_squared[:], mean_sb[:], mean_sb[:])

        num_ps = sum_banks.tile([C, N], F32, name="num_ps")
        count_ps = sum_banks.tile([CODES_HALF, HALVES], F32, name="count_ps")

        for b in range(NB):
            first_pixel = b // 2 * 2 * PB + b % 2
            pixels = slice(first_pixel, first_pixel + 2 * PB - 1, 2)

            half_ps = logit_banks.tile([PB, N], F32, name="half_ps")
            nc.tensor.matmul(half_ps[:], feat_sb[:, pixels], mean_sb[:], start=True, stop=False)
            nc.tensor.matmul(half_ps[:], minus_halves[:], mean_squared[:], start=False, stop=True)

            flipped_ps = flip_banks.tile([PB, C], BF16, name="flipped_ps")
            nc.tensor.transpose(flipped_ps[:], feat_sb[:, pixels], identity[:])
            flipped = flips.tile([PB, C], BF16, name="flipped")
            nc.scalar.copy(flipped[:], flipped_ps[:])

            logit = work.tile([PB, N], F32, name="logit")
            nc.vector.scalar_tensor_tensor(logit[:], half_ps[:], 2.0, adjust_sb[:, b, :], ALU.mult, ALU.subtract)
            minus_top = work.tile([PB, 1], F32, name="minus_top")
            nc.vector.tensor_reduce(minus_top[:], logit[:], mybir.AxisListType.X, ALU.max, negate=True)

            grown = work.tile([PB, N], F32, name="grown")
            row_sum = work.tile([PB, 1], F32, name="row_sum")
            nc.scalar.activation(grown[:], logit[:], ACT.Exp, bias=minus_top[:], scale=1.0, accum_out=row_sum[:])

            row_scale = work.tile([PB, 1], F32, name="row_scale")
            nc.vector.reciprocal(row_scale[:], row_sum[:])
            post = work.tile([PB, N], BF16, name="post")
            if b % 3 == 2:
                nc.scalar.activation(post[:], grown[:], ACT.Copy, scale=row_scale[:])
            elif b < NB - 1:
                nc.gpsimd.tensor_scalar(post[:], grown[:], row_scale[:], 1.0, ALU.mult, ALU.mult)
            else:
                nc.vector.tensor_scalar_mul(post[:], grown[:], row_scale[:])

            for h in range(HALVES):
                nc.tensor.matmul(
                    count_ps[:, h : h + 1],
                    post[:, h * CODES_HALF : (h + 1) * CODES_HALF],
                    one_column[:],
                    start=(b == 0 and h == 0),
                    stop=(b == NB - 1 and h == HALVES - 1),
                )
            nc.tensor.matmul(num_ps[:], flipped[:], post[:], start=(b == 0), stop=(b == NB - 1))

        r_column = held.tile([CODES_HALF, HALVES], F32, name="r_column")
        nc.vector.reciprocal(r_column[:], count_ps[:])
        num_sb = held.tile([C, N], F32, name="num_sb")
        nc.vector.tensor_copy(num_sb[:], num_ps[:])
        r_sb = held.tile([C, N], F32, name="r_sb")
        for h in range(HALVES):
            r_rows = flip_banks.tile([C, CODES_HALF], F32, name="r_rows", tag="flipped_ps")
            nc.tensor.transpose(r_rows[:], r_column[:, h : h + 1].to_broadcast([CODES_HALF, C]), identity_f32[:])
            nc.vector.tensor_copy(r_sb[:, h * CODES_HALF : (h + 1) * CODES_HALF], r_rows[:])

        nc.vector.tensor_tensor(window[:].indirect(offsets[:]), num_sb[:], r_sb[:], ALU.mult)

        for first in range(0, S, STORE_COLS):
            queue = nc.sync if (first // STORE_COLS) % 2 == 0 else nc.scalar
            queue.dma_start(out[:, first : first + STORE_COLS], window[:, first : first + STORE_COLS])
